import numpy as np
import ml_dtypes


def mxq(x, axis, fmt="e4m3"):
    dtype, down = {"e4m3": (ml_dtypes.float8_e4m3fn, 7), "e5m2": (ml_dtypes.float8_e5m2, 14)}[fmt]
    v = np.moveaxis(np.asarray(x, np.float32).astype(ml_dtypes.bfloat16).astype(np.float64), axis, -1)
    blocks = v.reshape(v.shape[:-1] + (-1, 32))
    amax = np.abs(blocks).max(-1, keepdims=True)
    byte = np.maximum(np.where(amax > 0, np.frexp(amax)[1] - 1 + 127, 0) - down, 1)
    scale = np.exp2(byte - 127.0)
    codes = (blocks / scale).astype(np.float32).astype(dtype).astype(np.float64)
    return np.moveaxis((codes * scale).reshape(v.shape), -1, axis)


WIDE = False


def mx_kscale(k):
    if not WIDE:
        return np.ones(k)
    levels = np.array([10, -10, 5, -5, 0])
    a = np.random.permutation(np.resize(levels, k // 512 * 4)).reshape(k // 512, 4)
    idx = np.arange(k)
    return np.exp2(a[idx // 512, idx % 128 // 32])


BF16 = ml_dtypes.bfloat16


def bf(x):
    return np.asarray(x, np.float32).astype(BF16)


def f64(x):
    return np.asarray(x).astype(np.float64)


B, D_IN, D_FEAT, N_EX, N_LAB = 128, 16384, 256, 512, 128
EPS = 1e-12


def l2_normalize(x):
    n = np.sqrt((x * x).sum(-1, keepdims=True))
    return x / np.maximum(n, EPS)


def setup_inputs():
    s = mx_kscale(D_IN)
    return {"features": bf(np.random.standard_normal((B, D_IN)) * s),
            "ex_features": bf(np.random.standard_normal((N_EX, D_IN)) * s),
            "g_weight": bf(np.random.standard_normal((D_FEAT, D_IN)) / np.sqrt(D_IN) / s)}


def reference(features, ex_features, g_weight):
    gq = mxq(f64(g_weight), 1, "e4m3")
    f = mxq(f64(features), 1, "e4m3") @ gq.T
    e = mxq(f64(ex_features), 1, "e4m3") @ gq.T
    return l2_normalize(f), l2_normalize(e)

@@ -1,0 +1,216 @@
+from contextlib import ExitStack
+
+import concourse.mybir as mybir
+from concourse.masks import make_identity
+
+F32 = mybir.dt.float32
+BF16 = mybir.dt.bfloat16
+U32 = mybir.dt.uint32
+U8 = mybir.dt.uint8
+FP8X4 = mybir.dt.float8_e4m3fn_x4
+ALU = mybir.AluOpType
+ACT = mybir.ActivationFunctionType
+
+P = 128
+B, N_EX, D_FEAT, D_IN = 128, 512, 256, 16384
+EPS = 1e-12
+FLOPS = 2 * (B + N_EX) * D_FEAT * D_IN
+
+K_PASS = 4 * P
+PASS_WORDS = K_PASS // 2
+BANK_WORDS = 512
+UNIT_BANKS = 4
+UNIT_VALUES = 2 * UNIT_BANKS * BANK_WORDS
+UNIT_CODES = UNIT_VALUES // 4
+
+RANGE_K = UNIT_VALUES
+RANGES = D_IN // RANGE_K
+X_PASSES = RANGE_K // K_PASS
+G_TILES = D_FEAT // P
+G_UNITS = G_TILES
+G_PASSES = X_PASSES // G_UNITS
+X_TILES = (B + N_EX) // P
+RANGE_UNITS = G_UNITS + X_TILES
+UNITS = RANGES * RANGE_UNITS
+
+ALL_PASSES = RANGES * X_TILES * X_PASSES
+
+RAW_BUFS = 12
+LAG = 4
+
+
+def passes_due(n):
+    return max(0, (n + 1 - LAG) * X_TILES * X_PASSES // RANGE_UNITS)
+
+
+def tile_minerva_pb_k_kernel(tc, features, ex_features, g_weight, out_0, out_1):
+    nc = tc.nc
+    with ExitStack() as ctx:
+        const = ctx.enter_context(tc.tile_pool(name="const", bufs=1))
+        raw_pool = ctx.enter_context(tc.tile_pool(name="raw", bufs=RAW_BUFS))
+        grouped_pool = ctx.enter_context(tc.tile_pool(name="grouped", bufs=3))
+        x_pool = ctx.enter_context(tc.tile_pool(name="x_mx", bufs=LAG))
+        g_pool = ctx.enter_context(tc.tile_pool(name="g_mx", bufs=2 * G_UNITS))
+        end_pool = ctx.enter_context(tc.tile_pool(name="end", bufs=3))
+        flip_psum = ctx.enter_context(tc.psum_pool(name="flip_psum", bufs=6))
+        acc_psum = ctx.enter_context(tc.psum_pool(name="acc_psum", bufs=2))
+
+        ident = const.tile([P, P], F32)
+        make_identity(nc, ident[:])
+
+        one = const.tile([P, 1], F32)
+        nc.vector.memset(one[:], 1.0)
+        one_root = const.tile([P, 1], F32)
+        nc.scalar.sqrt(one_root[:], one[:])
+
+        x_rows = [features] + [ex_features[t * P : (t + 1) * P, :] for t in range(N_EX // P)]
+        out_rows = [out_0] + [out_1[t * P : (t + 1) * P, :] for t in range(N_EX // P)]
+        g_rows = g_weight.rearrange("(j p) k -> p j k", p=P)
+        sums = [const.tile([P, D_FEAT], F32, name="sums%d" % i) for i in range(X_TILES)]
+
+        raw_of = {}
+        grouped_of = {}
+        mx_of = {}
+        acc_of = {}
+        sum_sq_of = {}
+        root_of = {}
+
+        def place(n):
+            return divmod(n, RANGE_UNITS)
+
+        def load(n):
+            s, m = place(n)
+            raw = raw_pool.tile([P, UNIT_VALUES], BF16)
+            if m < G_UNITS:
+                first = s * RANGE_K + m * (RANGE_K // G_UNITS)
+                nc.sync.dma_start(
+                    out=raw[:].rearrange("p (j k) -> p j k", j=G_TILES),
+                    in_=g_rows[:, :, first : first + RANGE_K // G_UNITS],
+                )
+            else:
+                nc.sync.dma_start(
+                    out=raw[:], in_=x_rows[m - G_UNITS][:, s * RANGE_K : (s + 1) * RANGE_K]
+                )
+            raw_of[n] = raw
+
+        def flip(n):
+            m = place(n)[1]
+            words = raw_of[n][:].bitcast(F32)
+            grouped = grouped_pool.tile([P, UNIT_VALUES], BF16, align_bytes=64)
+            grouped_words = grouped[:].bitcast(F32)
+            if m < G_UNITS:
+                bank_step, half_step = PASS_WORDS, UNIT_VALUES // 2 // G_TILES
+            else:
+                bank_step, half_step = 2 * PASS_WORDS, PASS_WORDS
+            for b in range(UNIT_BANKS):
+                bank = flip_psum.tile([P, BANK_WORDS], F32)
+                for h in range(2):
+                    for u in range(2):
+                        first = b * bank_step + h * half_step + u * P
+                        nc.tensor.transpose(
+                            bank[:, (2 * h + u) * P : (2 * h + u + 1) * P],
+                            words[:, first : first + P],
+                            ident[:],
+                        )
+                copy = nc.vector.tensor_copy if b == 0 else nc.scalar.copy
+                copy(
+                    out=grouped_words[:, b * BANK_WORDS : (b + 1) * BANK_WORDS].rearrange(
+                        "p (h r u) -> p h r u", h=2, u=2
+                    ),
+                    in_=bank[:].rearrange("p (h u r) -> p h r u", h=2, u=2),
+                )
+            grouped_of[n] = grouped
+
+        def quantise(n):
+            pool = g_pool if place(n)[1] < G_UNITS else x_pool
+            codes = pool.tile([P, UNIT_CODES], U32, align_bytes=64)
+            scales = pool.tile([P, UNIT_CODES], U8, align_bytes=64)
+            for half in range(2):
+                cols = slice(half * UNIT_CODES // 2, (half + 1) * UNIT_CODES // 2)
+                values = slice(half * UNIT_VALUES // 2, (half + 1) * UNIT_VALUES // 2)
+                nc.vector.quantize_mx(
+                    out=codes[:, cols].bitcast(FP8X4),
+                    scales=scales[:, cols],
+                    in_=grouped_of[n][:, values],
+                )
+            mx_of[n] = (codes, scales)
+
+        def multiply_pass(q):
+            s, rest = divmod(q, X_TILES * X_PASSES)
+            i, c = divmod(rest, X_PASSES)
+            n = s * RANGE_UNITS + G_UNITS + i
+            x_codes, x_scales = mx_of[n]
+            g_codes, g_scales = mx_of[s * RANGE_UNITS + c // G_PASSES]
+            if c == 0:
+                acc_of[n] = acc_psum.tile([P, D_FEAT], F32, name="acc")
+            acc = acc_of[n]
+            rows = slice(c * P, (c + 1) * P)
+            feats = slice((c % G_PASSES) * D_FEAT, (c % G_PASSES + 1) * D_FEAT)
+            nc.tensor.matmul_mx(
+                out=acc[:],
+                lhsT=x_codes[:, rows].bitcast(FP8X4),
+                lhsT_scale=x_scales[:, rows],
+                rhs=g_codes[:, feats].bitcast(FP8X4),
+                rhs_scale=g_scales[:, feats],
+                start=(c == 0),
+                stop=(c == X_PASSES - 1),
+            )
+            if c < X_PASSES - 1:
+                return
+            total = sums[i]
+            if s == 0:
+                nc.scalar.copy(out=total[:], in_=acc[:])
+            else:
+                nc.vector.tensor_tensor(out=total[:], in0=acc[:], in1=total[:], op=ALU.add)
+
+        def sum_squares(i):
+            squares = end_pool.tile([P, D_FEAT], F32)
+            sum_sq = end_pool.tile([P, 1], F32)
+            nc.scalar.activation(
+                out=squares[:], in_=sums[i][:], func=ACT.Square, accum_out=sum_sq[:]
+            )
+            sum_sq_of[i] = sum_sq
+
+        def root(i):
+            floored = end_pool.tile([P, 1], F32)
+            nc.vector.tensor_scalar(
+                out=floored[:], in0=sum_sq_of[i][:], scalar1=EPS * EPS, scalar2=None, op0=ALU.max
+            )
+            norm = end_pool.tile([P, 1], F32)
+            nc.scalar.sqrt(norm[:], floored[:])
+            root_of[i] = norm
+
+        def scale_and_store(i):
+            inverse = end_pool.tile([P, 1], F32)
+            nc.vector.reciprocal(inverse[:], root_of[i][:])
+            unit_rows = end_pool.tile([P, D_FEAT], F32)
+            nc.vector.tensor_scalar(
+                out=unit_rows[:], in0=sums[i][:], scalar1=inverse[:, 0:1], scalar2=None, op0=ALU.mult
+            )
+            nc.sync.dma_start(out=out_rows[i], in_=unit_rows[:])
+
+        with tc.manual_schedule():
+            for n in range(RAW_BUFS):
+                load(n)
+            done = 0
+            for n in range(UNITS):
+                flip(n)
+                if n + RAW_BUFS < UNITS:
+                    load(n + RAW_BUFS)
+                if n > 0:
+                    quantise(n - 1)
+                for q in range(done, passes_due(n)):
+                    multiply_pass(q)
+                done = passes_due(n)
+            quantise(UNITS - 1)
+            for i in range(X_TILES + 2):
+                if i < X_TILES:
+                    closed = ALL_PASSES - (X_TILES - 1 - i) * X_PASSES
+                    for q in range(done, closed):
+                        multiply_pass(q)
+                    done = max(done, closed)
+                    sum_squares(i)
+                if 1 <= i <= X_TILES:
+                    root(i - 1)
+                if i >= 2:
+                    scale_and_store(i - 2)

@@ -19,28 +19,80 @@ FLOPS = 2 * (B + N_EX) * D_FEAT * D_IN
 K_PASS = 4 * P
 PASS_WORDS = K_PASS // 2
 BANK_WORDS = 512
-UNIT_BANKS = 4
-UNIT_VALUES = 2 * UNIT_BANKS * BANK_WORDS
-UNIT_CODES = UNIT_VALUES // 4
+BANK_VALUES = 2 * BANK_WORDS
+CHUNK_BANKS = 2
+PASS_DELAY = 3
+RUN_BANKS = 4
+Q_DELAY = 1
 
-RANGE_K = UNIT_VALUES
-RANGES = D_IN // RANGE_K
-X_PASSES = RANGE_K // K_PASS
 G_TILES = D_FEAT // P
-G_UNITS = G_TILES
-G_PASSES = X_PASSES // G_UNITS
 X_TILES = (B + N_EX) // P
-RANGE_UNITS = G_UNITS + X_TILES
-UNITS = RANGES * RANGE_UNITS
+OPEN_TILES = 1
 
-ALL_PASSES = RANGES * X_TILES * X_PASSES
+RANGES = [2048, 2048, 4096, 4096, 4096]
+FIRST_G_K = 512
+G_K = 2048
+X_K = 4096
+LAST_X_K = 2048
 
 RAW_BUFS = 12
-LAG = 4
+LAG_BANKS = 10
+LEFT_PASSES = 23
 
 
-def passes_due(n):
-    return max(0, (n + 1 - LAG) * X_TILES * X_PASSES // RANGE_UNITS)
+def make_pieces():
+    g_pieces, x_tiles = [], []
+    start = 0
+    for s, range_k in enumerate(RANGES):
+        width = FIRST_G_K if s == 0 else G_K
+        g_pieces.append([(s, None, k, width) for k in range(start, start + range_k, width)])
+        tiles = []
+        for i in range(X_TILES):
+            last = s == len(RANGES) - 1 and i == X_TILES - 1
+            width = min(LAST_X_K if last else X_K, range_k)
+            tiles.append([(s, i, k, width) for k in range(start, start + range_k, width)])
+        x_tiles.append(tiles)
+        start += range_k
+    pieces = list(g_pieces[0])
+    for s in range(len(RANGES)):
+        coming = g_pieces[s + 1] if s + 1 < len(RANGES) else []
+        for i in range(X_TILES):
+            pieces += x_tiles[s][i]
+            pieces += coming[i * len(coming) // X_TILES : (i + 1) * len(coming) // X_TILES]
+    return pieces
+
+
+PIECES = make_pieces()
+
+
+def banks_of(n):
+    s, i, first, width = PIECES[n]
+    return width * (G_TILES if i is None else 1) // BANK_VALUES
+
+
+def stays_open(i):
+    return i >= X_TILES - OPEN_TILES
+
+
+def make_passes():
+    passes = []
+    for s in range(len(RANGES)):
+        for i in range(X_TILES):
+            group = []
+            for n, (ps, pi, first, width) in enumerate(PIECES):
+                if ps == s and pi == i:
+                    group += [(k, n) for k in range(first, first + width, K_PASS)]
+            for k, n in group:
+                passes.append((s, i, k, n, k == group[0][0], k == group[-1][0]))
+    return passes
+
+
+PASSES = make_passes()
+ALL_BANKS = sum(banks_of(n) for n in range(len(PIECES)))
+
+
+def passes_due(banks):
+    return max(0, (banks - LAG_BANKS) * (len(PASSES) - LEFT_PASSES) // (ALL_BANKS - LAG_BANKS))
 
 
 def tile_minerva_pb_k_kernel(tc, features, ex_features, g_weight, out_0, out_1):
@@ -49,10 +101,11 @@ def tile_minerva_pb_k_kernel(tc, features, ex_features, g_weight, out_0, out_1):
         const = ctx.enter_context(tc.tile_pool(name="const", bufs=1))
         raw_pool = ctx.enter_context(tc.tile_pool(name="raw", bufs=RAW_BUFS))
         grouped_pool = ctx.enter_context(tc.tile_pool(name="grouped", bufs=3))
-        x_pool = ctx.enter_context(tc.tile_pool(name="x_mx", bufs=LAG))
-        g_pool = ctx.enter_context(tc.tile_pool(name="g_mx", bufs=2 * G_UNITS))
-        end_pool = ctx.enter_context(tc.tile_pool(name="end", bufs=3))
-        flip_psum = ctx.enter_context(tc.psum_pool(name="flip_psum", bufs=6))
+        x_pool = ctx.enter_context(tc.tile_pool(name="x_mx", bufs=8))
+        g_pool = ctx.enter_context(tc.tile_pool(name="g_mx", bufs=8))
+        end_pool = ctx.enter_context(tc.tile_pool(name="end", bufs=X_TILES))
+        flip_psum = ctx.enter_context(tc.psum_pool(name="flip_psum", bufs=5))
+        last_psum = ctx.enter_context(tc.psum_pool(name="last_psum", bufs=1))
         acc_psum = ctx.enter_context(tc.psum_pool(name="acc_psum", bufs=2))
 
         ident = const.tile([P, P], F32)
@@ -61,101 +114,108 @@ def tile_minerva_pb_k_kernel(tc, features, ex_features, g_weight, out_0, out_1):
         one = const.tile([P, 1], F32)
         nc.vector.memset(one[:], 1.0)
         one_root = const.tile([P, 1], F32)
-        nc.scalar.sqrt(one_root[:], one[:])
+        nc.scalar.activation(out=one_root[:], in_=one[:], func=ACT.Abs_reciprocal_sqrt)
 
         x_rows = [features] + [ex_features[t * P : (t + 1) * P, :] for t in range(N_EX // P)]
         out_rows = [out_0] + [out_1[t * P : (t + 1) * P, :] for t in range(N_EX // P)]
         g_rows = g_weight.rearrange("(j p) k -> p j k", p=P)
-        sums = [const.tile([P, D_FEAT], F32, name="sums%d" % i) for i in range(X_TILES)]
+        sums = []
+        for i in range(X_TILES):
+            pool = last_psum if stays_open(i) else const
+            sums.append(pool.tile([P, D_FEAT], F32, name="sums%d" % i))
 
         raw_of = {}
         grouped_of = {}
         mx_of = {}
+        g_place = {}
         acc_of = {}
         sum_sq_of = {}
-        root_of = {}
+        inverse_of = {}
 
-        def place(n):
-            return divmod(n, RANGE_UNITS)
+        for n, (s, i, first, width) in enumerate(PIECES):
+            if i is None:
+                for c in range(width // K_PASS):
+                    g_place[first + c * K_PASS] = (n, c)
 
         def load(n):
-            s, m = place(n)
-            raw = raw_pool.tile([P, UNIT_VALUES], BF16)
-            if m < G_UNITS:
-                first = s * RANGE_K + m * (RANGE_K // G_UNITS)
+            s, i, first, width = PIECES[n]
+            raw = raw_pool.tile([P, banks_of(n) * BANK_VALUES], BF16)
+            if i is None:
                 nc.sync.dma_start(
                     out=raw[:].rearrange("p (j k) -> p j k", j=G_TILES),
-                    in_=g_rows[:, :, first : first + RANGE_K // G_UNITS],
+                    in_=g_rows[:, :, first : first + width],
                 )
             else:
-                nc.sync.dma_start(
-                    out=raw[:], in_=x_rows[m - G_UNITS][:, s * RANGE_K : (s + 1) * RANGE_K]
-                )
+                nc.sync.dma_start(out=raw[:], in_=x_rows[i][:, first : first + width])
             raw_of[n] = raw
 
-        def flip(n):
-            m = place(n)[1]
+        def flip(n, b, number):
+            s, i, first, width = PIECES[n]
+            banks = banks_of(n)
+            if b == 0:
+                grouped_of[n] = grouped_pool.tile(
+                    [P, banks * BANK_VALUES], BF16, name="grouped", align_bytes=64
+                )
+                pool = g_pool if i is None else x_pool
+                codes = pool.tile([P, banks * BANK_VALUES // 4], U32, align_bytes=64)
+                scales = pool.tile([P, banks * BANK_VALUES // 4], U8, align_bytes=64)
+                mx_of[n] = (codes, scales)
             words = raw_of[n][:].bitcast(F32)
-            grouped = grouped_pool.tile([P, UNIT_VALUES], BF16, align_bytes=64)
-            grouped_words = grouped[:].bitcast(F32)
-            if m < G_UNITS:
-                bank_step, half_step = PASS_WORDS, UNIT_VALUES // 2 // G_TILES
+            grouped_words = grouped_of[n][:].bitcast(F32)
+            if i is None:
+                bank_step, half_step = PASS_WORDS, width // 2
             else:
                 bank_step, half_step = 2 * PASS_WORDS, PASS_WORDS
-            for b in range(UNIT_BANKS):
-                bank = flip_psum.tile([P, BANK_WORDS], F32)
-                for h in range(2):
-                    for u in range(2):
-                        first = b * bank_step + h * half_step + u * P
-                        nc.tensor.transpose(
-                            bank[:, (2 * h + u) * P : (2 * h + u + 1) * P],
-                            words[:, first : first + P],
-                            ident[:],
-                        )
-                copy = nc.vector.tensor_copy if b == 0 else nc.scalar.copy
-                copy(
-                    out=grouped_words[:, b * BANK_WORDS : (b + 1) * BANK_WORDS].rearrange(
-                        "p (h r u) -> p h r u", h=2, u=2
-                    ),
-                    in_=bank[:].rearrange("p (h u r) -> p h r u", h=2, u=2),
-                )
-            grouped_of[n] = grouped
+            bank = flip_psum.tile([P, BANK_WORDS], F32)
+            for h in range(2):
+                for u in range(2):
+                    at = b * bank_step + h * half_step + u * P
+                    nc.tensor.transpose(
+                        bank[:, (2 * h + u) * P : (2 * h + u + 1) * P],
+                        words[:, at : at + P],
+                        ident[:],
+                    )
+            copy = nc.vector.tensor_copy if number % 4 == 0 else nc.scalar.copy
+            copy(
+                out=grouped_words[:, b * BANK_WORDS : (b + 1) * BANK_WORDS].rearrange(
+                    "p (h r u) -> p h r u", h=2, u=2
+                ),
+                in_=bank[:].rearrange("p (h u r) -> p h r u", h=2, u=2),
+            )
 
-        def quantise(n):
-            pool = g_pool if place(n)[1] < G_UNITS else x_pool
-            codes = pool.tile([P, UNIT_CODES], U32, align_bytes=64)
-            scales = pool.tile([P, UNIT_CODES], U8, align_bytes=64)
-            for half in range(2):
-                cols = slice(half * UNIT_CODES // 2, (half + 1) * UNIT_CODES // 2)
-                values = slice(half * UNIT_VALUES // 2, (half + 1) * UNIT_VALUES // 2)
-                nc.vector.quantize_mx(
-                    out=codes[:, cols].bitcast(FP8X4),
-                    scales=scales[:, cols],
-                    in_=grouped_of[n][:, values],
-                )
-            mx_of[n] = (codes, scales)
+        def quantise(n, b, banks):
+            codes, scales = mx_of[n]
+            at, end = b * BANK_VALUES, (b + banks) * BANK_VALUES
+            nc.vector.quantize_mx(
+                out=codes[:, at // 4 : end // 4].bitcast(FP8X4),
+                scales=scales[:, at // 4 : end // 4],
+                in_=grouped_of[n][:, at:end],
+            )
 
         def multiply_pass(q):
-            s, rest = divmod(q, X_TILES * X_PASSES)
-            i, c = divmod(rest, X_PASSES)
-            n = s * RANGE_UNITS + G_UNITS + i
+            s, i, k, n, opens, closes = PASSES[q]
             x_codes, x_scales = mx_of[n]
-            g_codes, g_scales = mx_of[s * RANGE_UNITS + c // G_PASSES]
-            if c == 0:
-                acc_of[n] = acc_psum.tile([P, D_FEAT], F32, name="acc")
-            acc = acc_of[n]
-            rows = slice(c * P, (c + 1) * P)
-            feats = slice((c % G_PASSES) * D_FEAT, (c % G_PASSES + 1) * D_FEAT)
+            g_n, g_c = g_place[k]
+            g_codes, g_scales = mx_of[g_n]
+            if stays_open(i):
+                opens, closes = opens and s == 0, closes and s == len(RANGES) - 1
+                acc_of[i] = sums[i]
+            elif opens:
+                acc_of[i] = acc_psum.tile([P, D_FEAT], F32, name="acc")
+            acc = acc_of[i]
+            x_c = (k - PIECES[n][2]) // K_PASS
+            rows = slice(x_c * P, (x_c + 1) * P)
+            feats = slice(g_c * D_FEAT, (g_c + 1) * D_FEAT)
             nc.tensor.matmul_mx(
                 out=acc[:],
                 lhsT=x_codes[:, rows].bitcast(FP8X4),
                 lhsT_scale=x_scales[:, rows],
                 rhs=g_codes[:, feats].bitcast(FP8X4),
                 rhs_scale=g_scales[:, feats],
-                start=(c == 0),
-                stop=(c == X_PASSES - 1),
+                start=opens,
+                stop=closes,
             )
-            if c < X_PASSES - 1:
+            if stays_open(i) or not closes:
                 return
             total = sums[i]
             if s == 0:
@@ -171,21 +231,23 @@ def tile_minerva_pb_k_kernel(tc, features, ex_features, g_weight, out_0, out_1):
             )
             sum_sq_of[i] = sum_sq
 
-        def root(i):
+        def invert(i):
             floored = end_pool.tile([P, 1], F32)
             nc.vector.tensor_scalar(
                 out=floored[:], in0=sum_sq_of[i][:], scalar1=EPS * EPS, scalar2=None, op0=ALU.max
             )
-            norm = end_pool.tile([P, 1], F32)
-            nc.scalar.sqrt(norm[:], floored[:])
-            root_of[i] = norm
+            inverse = end_pool.tile([P, 1], F32)
+            nc.scalar.activation(out=inverse[:], in_=floored[:], func=ACT.Abs_reciprocal_sqrt)
+            inverse_of[i] = inverse
 
         def scale_and_store(i):
-            inverse = end_pool.tile([P, 1], F32)
-            nc.vector.reciprocal(inverse[:], root_of[i][:])
             unit_rows = end_pool.tile([P, D_FEAT], F32)
             nc.vector.tensor_scalar(
-                out=unit_rows[:], in0=sums[i][:], scalar1=inverse[:, 0:1], scalar2=None, op0=ALU.mult
+                out=unit_rows[:],
+                in0=sums[i][:],
+                scalar1=inverse_of[i][:, 0:1],
+                scalar2=None,
+                op0=ALU.mult,
             )
             nc.sync.dma_start(out=out_rows[i], in_=unit_rows[:])
 
@@ -193,24 +255,54 @@ def tile_minerva_pb_k_kernel(tc, features, ex_features, g_weight, out_0, out_1):
             for n in range(RAW_BUFS):
                 load(n)
             done = 0
-            for n in range(UNITS):
-                flip(n)
-                if n + RAW_BUFS < UNITS:
-                    load(n + RAW_BUFS)
-                if n > 0:
-                    quantise(n - 1)
-                for q in range(done, passes_due(n)):
-                    multiply_pass(q)
-                done = passes_due(n)
-            quantise(UNITS - 1)
+            number = 0
+            waiting = []
+            quantised = {}
+
+            def quantise_waiting(number):
+                for entry in list(waiting):
+                    if entry[0] > number:
+                        continue
+                    waiting.remove(entry)
+                    n, b, banks = entry[1:]
+                    quantise(n, b, banks)
+                    for m in range(b, b + banks):
+                        quantised[n, m] = number
+
+            def is_ready(q):
+                s, i, k, n = PASSES[q][:4]
+                g_n, g_c = g_place[k]
+                x_bank = (n, (k - PIECES[n][2]) // BANK_VALUES)
+                at = max(quantised.get(x_bank, ALL_BANKS), quantised.get((g_n, g_c), ALL_BANKS))
+                return at + PASS_DELAY <= number
+
+            for n in range(len(PIECES)):
+                chunk = min(banks_of(n), CHUNK_BANKS)
+                for b in range(banks_of(n)):
+                    flip(n, b, number)
+                    number += 1
+                    quantise_waiting(number)
+                    if (b + 1) % chunk == 0:
+                        waiting.append((number + Q_DELAY, n, b + 1 - chunk, chunk))
+                        quantise_waiting(number)
+                    if b == banks_of(n) - 1 and n + RAW_BUFS < len(PIECES):
+                        load(n + RAW_BUFS)
+                    if number % RUN_BANKS == 0:
+                        due = max(done, passes_due(number))
+                        if PIECES[n][0] == 0 or PASSES[done][0] == 0:
+                            due = len(PASSES)
+                        while done < due and is_ready(done):
+                            multiply_pass(done)
+                            done += 1
+            quantise_waiting(ALL_BANKS + Q_DELAY)
             for i in range(X_TILES + 2):
                 if i < X_TILES:
-                    closed = ALL_PASSES - (X_TILES - 1 - i) * X_PASSES
+                    closed = max(q for q, p in enumerate(PASSES) if p[1] == i) + 1
                     for q in range(done, closed):
                         multiply_pass(q)
                     done = max(done, closed)
                     sum_squares(i)
                 if 1 <= i <= X_TILES:
-                    root(i - 1)
+                    invert(i - 1)
                 if i >= 2:
                     scale_and_store(i - 2)

@@ -31,11 +31,11 @@ OPEN_TILES = 1
 
 RANGES = [2048, 2048, 4096, 4096, 4096]
 FIRST_G_K = 512
-G_K = 2048
-X_K = 4096
+G_K = 1024
+X_K = 2048
 LAST_X_K = 2048
 
-RAW_BUFS = 12
+RAW_BUFS = 24
 LAG_BANKS = 10
 LEFT_PASSES = 23
 
@@ -100,9 +100,9 @@ def tile_minerva_pb_k_kernel(tc, features, ex_features, g_weight, out_0, out_1):
     with ExitStack() as ctx:
         const = ctx.enter_context(tc.tile_pool(name="const", bufs=1))
         raw_pool = ctx.enter_context(tc.tile_pool(name="raw", bufs=RAW_BUFS))
-        grouped_pool = ctx.enter_context(tc.tile_pool(name="grouped", bufs=3))
-        x_pool = ctx.enter_context(tc.tile_pool(name="x_mx", bufs=8))
-        g_pool = ctx.enter_context(tc.tile_pool(name="g_mx", bufs=8))
+        grouped_pool = ctx.enter_context(tc.tile_pool(name="grouped", bufs=5))
+        x_pool = ctx.enter_context(tc.tile_pool(name="x_mx", bufs=12))
+        g_pool = ctx.enter_context(tc.tile_pool(name="g_mx", bufs=16))
         end_pool = ctx.enter_context(tc.tile_pool(name="end", bufs=X_TILES))
         flip_psum = ctx.enter_context(tc.psum_pool(name="flip_psum", bufs=5))
         last_psum = ctx.enter_context(tc.psum_pool(name="last_psum", bufs=1))

@@ -21,34 +21,36 @@ PASS_WORDS = K_PASS // 2
 BANK_WORDS = 512
 BANK_VALUES = 2 * BANK_WORDS
 CHUNK_BANKS = 2
-PASS_DELAY = 3
-RUN_BANKS = 4
-Q_DELAY = 1
 
 G_TILES = D_FEAT // P
 X_TILES = (B + N_EX) // P
-OPEN_TILES = 1
+LAST_TILE = X_TILES - 1
 
-RANGES = [2048, 2048, 4096, 4096, 4096]
+RANGES = [1024] * 2 + [2048] * 7
 FIRST_G_K = 512
 G_K = 1024
 X_K = 2048
-LAST_X_K = 2048
+LAST_X_K = 1024
 
 RAW_BUFS = 24
-LAG_BANKS = 10
-LEFT_PASSES = 23
+RUN_BANKS = 4
+Q_DELAY = 1
+PASS_DELAY = 4
+LAG_BANKS = 6
+LEFT_PASSES = 16
+HELD_RANGES = 2
+VECTOR_BANKS, ALL_SHARES = 1, 4
 
 
 def make_pieces():
     g_pieces, x_tiles = [], []
     start = 0
     for s, range_k in enumerate(RANGES):
-        width = FIRST_G_K if s == 0 else G_K
+        width = min(FIRST_G_K if s == 0 else G_K, range_k)
         g_pieces.append([(s, None, k, width) for k in range(start, start + range_k, width)])
         tiles = []
         for i in range(X_TILES):
-            last = s == len(RANGES) - 1 and i == X_TILES - 1
+            last = s == len(RANGES) - 1 and i == LAST_TILE
             width = min(LAST_X_K if last else X_K, range_k)
             tiles.append([(s, i, k, width) for k in range(start, start + range_k, width)])
         x_tiles.append(tiles)
@@ -70,25 +72,23 @@ def banks_of(n):
     return width * (G_TILES if i is None else 1) // BANK_VALUES
 
 
-def stays_open(i):
-    return i >= X_TILES - OPEN_TILES
-
-
 def make_passes():
-    passes = []
+    passes, held = [], []
     for s in range(len(RANGES)):
         for i in range(X_TILES):
-            group = []
             for n, (ps, pi, first, width) in enumerate(PIECES):
                 if ps == s and pi == i:
-                    group += [(k, n) for k in range(first, first + width, K_PASS)]
-            for k, n in group:
-                passes.append((s, i, k, n, k == group[0][0], k == group[-1][0]))
-    return passes
+                    at_end = i == LAST_TILE and s >= len(RANGES) - HELD_RANGES
+                    for k in range(first, first + width, K_PASS):
+                        (held if at_end else passes).append((i, k, n))
+    return passes + held
 
 
 PASSES = make_passes()
 ALL_BANKS = sum(banks_of(n) for n in range(len(PIECES)))
+PAIRS = (X_TILES + 1) // 2
+FIRST_PASS = [min(q for q, p in enumerate(PASSES) if p[0] // 2 == j) for j in range(PAIRS)]
+LAST_PASS = [max(q for q, p in enumerate(PASSES) if p[0] // 2 == j) for j in range(PAIRS)]
 
 
 def passes_due(banks):
@@ -100,13 +100,12 @@ def tile_minerva_pb_k_kernel(tc, features, ex_features, g_weight, out_0, out_1):
     with ExitStack() as ctx:
         const = ctx.enter_context(tc.tile_pool(name="const", bufs=1))
         raw_pool = ctx.enter_context(tc.tile_pool(name="raw", bufs=RAW_BUFS))
-        grouped_pool = ctx.enter_context(tc.tile_pool(name="grouped", bufs=5))
-        x_pool = ctx.enter_context(tc.tile_pool(name="x_mx", bufs=12))
-        g_pool = ctx.enter_context(tc.tile_pool(name="g_mx", bufs=16))
+        grouped_pool = ctx.enter_context(tc.tile_pool(name="grouped", bufs=6))
+        x_pool = ctx.enter_context(tc.tile_pool(name="x_mx", bufs=14))
+        g_pool = ctx.enter_context(tc.tile_pool(name="g_mx", bufs=14))
         end_pool = ctx.enter_context(tc.tile_pool(name="end", bufs=X_TILES))
         flip_psum = ctx.enter_context(tc.psum_pool(name="flip_psum", bufs=5))
-        last_psum = ctx.enter_context(tc.psum_pool(name="last_psum", bufs=1))
-        acc_psum = ctx.enter_context(tc.psum_pool(name="acc_psum", bufs=2))
+        sums_psum = ctx.enter_context(tc.psum_pool(name="sums_psum", bufs=1))
 
         ident = const.tile([P, P], F32)
         make_identity(nc, ident[:])
@@ -120,15 +119,14 @@ def tile_minerva_pb_k_kernel(tc, features, ex_features, g_weight, out_0, out_1):
         out_rows = [out_0] + [out_1[t * P : (t + 1) * P, :] for t in range(N_EX // P)]
         g_rows = g_weight.rearrange("(j p) k -> p j k", p=P)
         sums = []
-        for i in range(X_TILES):
-            pool = last_psum if stays_open(i) else const
-            sums.append(pool.tile([P, D_FEAT], F32, name="sums%d" % i))
+        for pair in range(PAIRS):
+            bank = sums_psum.tile([P, BANK_WORDS], F32, name="sums%d" % pair)
+            sums += [bank[:, :D_FEAT], bank[:, D_FEAT:]]
 
         raw_of = {}
         grouped_of = {}
         mx_of = {}
         g_place = {}
-        acc_of = {}
         sum_sq_of = {}
         inverse_of = {}
 
@@ -175,7 +173,8 @@ def tile_minerva_pb_k_kernel(tc, features, ex_features, g_weight, out_0, out_1):
                         words[:, at : at + P],
                         ident[:],
                     )
-            copy = nc.vector.tensor_copy if number % 4 == 0 else nc.scalar.copy
+            on_vector = number * VECTOR_BANKS % ALL_SHARES < VECTOR_BANKS
+            copy = nc.vector.tensor_copy if on_vector else nc.scalar.copy
             copy(
                 out=grouped_words[:, b * BANK_WORDS : (b + 1) * BANK_WORDS].rearrange(
                     "p (h r u) -> p h r u", h=2, u=2
@@ -193,41 +192,28 @@ def tile_minerva_pb_k_kernel(tc, features, ex_features, g_weight, out_0, out_1):
             )
 
         def multiply_pass(q):
-            s, i, k, n, opens, closes = PASSES[q]
+            i, k, n = PASSES[q]
             x_codes, x_scales = mx_of[n]
             g_n, g_c = g_place[k]
             g_codes, g_scales = mx_of[g_n]
-            if stays_open(i):
-                opens, closes = opens and s == 0, closes and s == len(RANGES) - 1
-                acc_of[i] = sums[i]
-            elif opens:
-                acc_of[i] = acc_psum.tile([P, D_FEAT], F32, name="acc")
-            acc = acc_of[i]
             x_c = (k - PIECES[n][2]) // K_PASS
             rows = slice(x_c * P, (x_c + 1) * P)
             feats = slice(g_c * D_FEAT, (g_c + 1) * D_FEAT)
             nc.tensor.matmul_mx(
-                out=acc[:],
+                out=sums[i],
                 lhsT=x_codes[:, rows].bitcast(FP8X4),
                 lhsT_scale=x_scales[:, rows],
                 rhs=g_codes[:, feats].bitcast(FP8X4),
                 rhs_scale=g_scales[:, feats],
-                start=opens,
-                stop=closes,
+                start=(q in FIRST_PASS),
+                stop=(q in LAST_PASS),
             )
-            if stays_open(i) or not closes:
-                return
-            total = sums[i]
-            if s == 0:
-                nc.scalar.copy(out=total[:], in_=acc[:])
-            else:
-                nc.vector.tensor_tensor(out=total[:], in0=acc[:], in1=total[:], op=ALU.add)
 
         def sum_squares(i):
             squares = end_pool.tile([P, D_FEAT], F32)
             sum_sq = end_pool.tile([P, 1], F32)
             nc.scalar.activation(
-                out=squares[:], in_=sums[i][:], func=ACT.Square, accum_out=sum_sq[:]
+                out=squares[:], in_=sums[i], func=ACT.Square, accum_out=sum_sq[:]
             )
             sum_sq_of[i] = sum_sq
 
@@ -244,7 +230,7 @@ def tile_minerva_pb_k_kernel(tc, features, ex_features, g_weight, out_0, out_1):
             unit_rows = end_pool.tile([P, D_FEAT], F32)
             nc.vector.tensor_scalar(
                 out=unit_rows[:],
-                in0=sums[i][:],
+                in0=sums[i],
                 scalar1=inverse_of[i][:, 0:1],
                 scalar2=None,
                 op0=ALU.mult,
@@ -270,39 +256,41 @@ def tile_minerva_pb_k_kernel(tc, features, ex_features, g_weight, out_0, out_1):
                         quantised[n, m] = number
 
             def is_ready(q):
-                s, i, k, n = PASSES[q][:4]
-                g_n, g_c = g_place[k]
+                i, k, n = PASSES[q]
                 x_bank = (n, (k - PIECES[n][2]) // BANK_VALUES)
-                at = max(quantised.get(x_bank, ALL_BANKS), quantised.get((g_n, g_c), ALL_BANKS))
+                at = max(quantised.get(x_bank, ALL_BANKS), quantised.get(g_place[k], ALL_BANKS))
                 return at + PASS_DELAY <= number
 
             for n in range(len(PIECES)):
                 chunk = min(banks_of(n), CHUNK_BANKS)
+                in_last = PIECES[n][0] == len(RANGES) - 1
                 for b in range(banks_of(n)):
                     flip(n, b, number)
                     number += 1
                     quantise_waiting(number)
                     if (b + 1) % chunk == 0:
                         waiting.append((number + Q_DELAY, n, b + 1 - chunk, chunk))
-                        quantise_waiting(number)
                     if b == banks_of(n) - 1 and n + RAW_BUFS < len(PIECES):
                         load(n + RAW_BUFS)
                     if number % RUN_BANKS == 0:
-                        due = max(done, passes_due(number))
-                        if PIECES[n][0] == 0 or PASSES[done][0] == 0:
+                        due = passes_due(number)
+                        if PIECES[PASSES[done][2]][0] == 0:
                             due = len(PASSES)
                         while done < due and is_ready(done):
                             multiply_pass(done)
                             done += 1
             quantise_waiting(ALL_BANKS + Q_DELAY)
-            for i in range(X_TILES + 2):
-                if i < X_TILES:
-                    closed = max(q for q, p in enumerate(PASSES) if p[1] == i) + 1
-                    for q in range(done, closed):
+            tiles_of = [[i for i in range(X_TILES) if i // 2 == j] for j in range(PAIRS)]
+            for j in range(PAIRS + 2):
+                if j < PAIRS:
+                    for q in range(done, LAST_PASS[j] + 1):
                         multiply_pass(q)
-                    done = max(done, closed)
-                    sum_squares(i)
-                if 1 <= i <= X_TILES:
-                    invert(i - 1)
-                if i >= 2:
-                    scale_and_store(i - 2)
+                    done = max(done, LAST_PASS[j] + 1)
+                    for i in tiles_of[j]:
+                        sum_squares(i)
+                if 1 <= j <= PAIRS:
+                    for i in tiles_of[j - 1]:
+                        invert(i)
+                if j >= 2:
+                    for i in tiles_of[j - 2]:
+                        scale_and_store(i)

@@ -26,8 +26,8 @@ G_TILES = D_FEAT // P
 X_TILES = (B + N_EX) // P
 LAST_TILE = X_TILES - 1
 
-RANGES = [1024] * 2 + [2048] * 7
-FIRST_G_K = 512
+RANGES = [2048] * 8
+FIRST_G_K = 1024
 G_K = 1024
 X_K = 2048
 LAST_X_K = 1024
@@ -36,9 +36,9 @@ RAW_BUFS = 24
 RUN_BANKS = 4
 Q_DELAY = 1
 PASS_DELAY = 4
-LAG_BANKS = 6
-LEFT_PASSES = 16
-HELD_RANGES = 2
+LAG_BANKS = 8
+LEFT_PASSES = 12
+HELD_RANGES = 1
 VECTOR_BANKS, ALL_SHARES = 1, 4
 
 

from contextlib import ExitStack

import concourse.mybir as mybir
from concourse.masks import make_identity

F32 = mybir.dt.float32
BF16 = mybir.dt.bfloat16
U32 = mybir.dt.uint32
U8 = mybir.dt.uint8
FP8X4 = mybir.dt.float8_e4m3fn_x4
ALU = mybir.AluOpType
ACT = mybir.ActivationFunctionType

P = 128
B, N_EX, D_FEAT, D_IN = 128, 512, 256, 16384
EPS = 1e-12
FLOPS = 2 * (B + N_EX) * D_FEAT * D_IN

K_PASS = 4 * P
PASS_WORDS = K_PASS // 2
BANK_WORDS = 512
BANK_VALUES = 2 * BANK_WORDS
CHUNK_BANKS = 2

G_TILES = D_FEAT // P
X_TILES = (B + N_EX) // P
LAST_TILE = X_TILES - 1

RANGES = [2048] * 8
FIRST_G_K = 1024
G_K = 1024
X_K = 2048
LAST_X_K = 1024

RAW_BUFS = 24
RUN_BANKS = 4
Q_DELAY = 1
PASS_DELAY = 4
LAG_BANKS = 8
LEFT_PASSES = 12
HELD_RANGES = 1
VECTOR_BANKS, ALL_SHARES = 1, 4


def make_pieces():
    g_pieces, x_tiles = [], []
    start = 0
    for s, range_k in enumerate(RANGES):
        width = min(FIRST_G_K if s == 0 else G_K, range_k)
        g_pieces.append([(s, None, k, width) for k in range(start, start + range_k, width)])
        tiles = []
        for i in range(X_TILES):
            last = s == len(RANGES) - 1 and i == LAST_TILE
            width = min(LAST_X_K if last else X_K, range_k)
            tiles.append([(s, i, k, width) for k in range(start, start + range_k, width)])
        x_tiles.append(tiles)
        start += range_k
    pieces = list(g_pieces[0])
    for s in range(len(RANGES)):
        coming = g_pieces[s + 1] if s + 1 < len(RANGES) else []
        for i in range(X_TILES):
            pieces += x_tiles[s][i]
            pieces += coming[i * len(coming) // X_TILES : (i + 1) * len(coming) // X_TILES]
    return pieces


PIECES = make_pieces()


def banks_of(n):
    s, i, first, width = PIECES[n]
    return width * (G_TILES if i is None else 1) // BANK_VALUES


def make_passes():
    passes, held = [], []
    for s in range(len(RANGES)):
        for i in range(X_TILES):
            for n, (ps, pi, first, width) in enumerate(PIECES):
                if ps == s and pi == i:
                    at_end = i == LAST_TILE and s >= len(RANGES) - HELD_RANGES
                    for k in range(first, first + width, K_PASS):
                        (held if at_end else passes).append((i, k, n))
    return passes + held


PASSES = make_passes()
ALL_BANKS = sum(banks_of(n) for n in range(len(PIECES)))
PAIRS = (X_TILES + 1) // 2
FIRST_PASS = [min(q for q, p in enumerate(PASSES) if p[0] // 2 == j) for j in range(PAIRS)]
LAST_PASS = [max(q for q, p in enumerate(PASSES) if p[0] // 2 == j) for j in range(PAIRS)]


def passes_due(banks):
    return max(0, (banks - LAG_BANKS) * (len(PASSES) - LEFT_PASSES) // (ALL_BANKS - LAG_BANKS))


def tile_minerva_pb_k_kernel(tc, features, ex_features, g_weight, out_0, out_1):
    nc = tc.nc
    with ExitStack() as ctx:
        const = ctx.enter_context(tc.tile_pool(name="const", bufs=1))
        raw_pool = ctx.enter_context(tc.tile_pool(name="raw", bufs=RAW_BUFS))
        grouped_pool = ctx.enter_context(tc.tile_pool(name="grouped", bufs=6))
        x_pool = ctx.enter_context(tc.tile_pool(name="x_mx", bufs=14))
        g_pool = ctx.enter_context(tc.tile_pool(name="g_mx", bufs=14))
        end_pool = ctx.enter_context(tc.tile_pool(name="end", bufs=X_TILES))
        flip_psum = ctx.enter_context(tc.psum_pool(name="flip_psum", bufs=5))
        sums_psum = ctx.enter_context(tc.psum_pool(name="sums_psum", bufs=1))

        ident = const.tile([P, P], F32)
        make_identity(nc, ident[:])

        one = const.tile([P, 1], F32)
        nc.vector.memset(one[:], 1.0)
        one_root = const.tile([P, 1], F32)
        nc.scalar.activation(out=one_root[:], in_=one[:], func=ACT.Abs_reciprocal_sqrt)

        x_rows = [features] + [ex_features[t * P : (t + 1) * P, :] for t in range(N_EX // P)]
        out_rows = [out_0] + [out_1[t * P : (t + 1) * P, :] for t in range(N_EX // P)]
        g_rows = g_weight.rearrange("(j p) k -> p j k", p=P)
        sums = []
        for pair in range(PAIRS):
            bank = sums_psum.tile([P, BANK_WORDS], F32, name="sums%d" % pair)
            sums += [bank[:, :D_FEAT], bank[:, D_FEAT:]]

        raw_of = {}
        grouped_of = {}
        mx_of = {}
        g_place = {}
        sum_sq_of = {}
        inverse_of = {}

        for n, (s, i, first, width) in enumerate(PIECES):
            if i is None:
                for c in range(width // K_PASS):
                    g_place[first + c * K_PASS] = (n, c)

        def load(n):
            s, i, first, width = PIECES[n]
            raw = raw_pool.tile([P, banks_of(n) * BANK_VALUES], BF16)
            if i is None:
                nc.sync.dma_start(
                    out=raw[:].rearrange("p (j k) -> p j k", j=G_TILES),
                    in_=g_rows[:, :, first : first + width],
                )
            else:
                nc.sync.dma_start(out=raw[:], in_=x_rows[i][:, first : first + width])
            raw_of[n] = raw

        def flip(n, b, number):
            s, i, first, width = PIECES[n]
            banks = banks_of(n)
            if b == 0:
                grouped_of[n] = grouped_pool.tile(
                    [P, banks * BANK_VALUES], BF16, name="grouped", align_bytes=64
                )
                pool = g_pool if i is None else x_pool
                codes = pool.tile([P, banks * BANK_VALUES // 4], U32, align_bytes=64)
                scales = pool.tile([P, banks * BANK_VALUES // 4], U8, align_bytes=64)
                mx_of[n] = (codes, scales)
            words = raw_of[n][:].bitcast(F32)
            grouped_words = grouped_of[n][:].bitcast(F32)
            if i is None:
                bank_step, half_step = PASS_WORDS, width // 2
            else:
                bank_step, half_step = 2 * PASS_WORDS, PASS_WORDS
            bank = flip_psum.tile([P, BANK_WORDS], F32)
            for h in range(2):
                for u in range(2):
                    at = b * bank_step + h * half_step + u * P
                    nc.tensor.transpose(
                        bank[:, (2 * h + u) * P : (2 * h + u + 1) * P],
                        words[:, at : at + P],
                        ident[:],
                    )
            on_vector = number * VECTOR_BANKS % ALL_SHARES < VECTOR_BANKS
            copy = nc.vector.tensor_copy if on_vector else nc.scalar.copy
            copy(
                out=grouped_words[:, b * BANK_WORDS : (b + 1) * BANK_WORDS].rearrange(
                    "p (h r u) -> p h r u", h=2, u=2
                ),
                in_=bank[:].rearrange("p (h u r) -> p h r u", h=2, u=2),
            )

        def quantise(n, b, banks):
            codes, scales = mx_of[n]
            at, end = b * BANK_VALUES, (b + banks) * BANK_VALUES
            nc.vector.quantize_mx(
                out=codes[:, at // 4 : end // 4].bitcast(FP8X4),
                scales=scales[:, at // 4 : end // 4],
                in_=grouped_of[n][:, at:end],
            )

        def multiply_pass(q):
            i, k, n = PASSES[q]
            x_codes, x_scales = mx_of[n]
            g_n, g_c = g_place[k]
            g_codes, g_scales = mx_of[g_n]
            x_c = (k - PIECES[n][2]) // K_PASS
            rows = slice(x_c * P, (x_c + 1) * P)
            feats = slice(g_c * D_FEAT, (g_c + 1) * D_FEAT)
            nc.tensor.matmul_mx(
                out=sums[i],
                lhsT=x_codes[:, rows].bitcast(FP8X4),
                lhsT_scale=x_scales[:, rows],
                rhs=g_codes[:, feats].bitcast(FP8X4),
                rhs_scale=g_scales[:, feats],
                start=(q in FIRST_PASS),
                stop=(q in LAST_PASS),
            )

        def sum_squares(i):
            squares = end_pool.tile([P, D_FEAT], F32)
            sum_sq = end_pool.tile([P, 1], F32)
            nc.scalar.activation(
                out=squares[:], in_=sums[i], func=ACT.Square, accum_out=sum_sq[:]
            )
            sum_sq_of[i] = sum_sq

        def invert(i):
            floored = end_pool.tile([P, 1], F32)
            nc.vector.tensor_scalar(
                out=floored[:], in0=sum_sq_of[i][:], scalar1=EPS * EPS, scalar2=None, op0=ALU.max
            )
            inverse = end_pool.tile([P, 1], F32)
            nc.scalar.activation(out=inverse[:], in_=floored[:], func=ACT.Abs_reciprocal_sqrt)
            inverse_of[i] = inverse

        def scale_and_store(i):
            unit_rows = end_pool.tile([P, D_FEAT], F32)
            nc.vector.tensor_scalar(
                out=unit_rows[:],
                in0=sums[i],
                scalar1=inverse_of[i][:, 0:1],
                scalar2=None,
                op0=ALU.mult,
            )
            nc.sync.dma_start(out=out_rows[i], in_=unit_rows[:])

        with tc.manual_schedule():
            for n in range(RAW_BUFS):
                load(n)
            done = 0
            number = 0
            waiting = []
            quantised = {}

            def quantise_waiting(number):
                for entry in list(waiting):
                    if entry[0] > number:
                        continue
                    waiting.remove(entry)
                    n, b, banks = entry[1:]
                    quantise(n, b, banks)
                    for m in range(b, b + banks):
                        quantised[n, m] = number

            def is_ready(q):
                i, k, n = PASSES[q]
                x_bank = (n, (k - PIECES[n][2]) // BANK_VALUES)
                at = max(quantised.get(x_bank, ALL_BANKS), quantised.get(g_place[k], ALL_BANKS))
                return at + PASS_DELAY <= number

            for n in range(len(PIECES)):
                chunk = min(banks_of(n), CHUNK_BANKS)
                in_last = PIECES[n][0] == len(RANGES) - 1
                for b in range(banks_of(n)):
                    flip(n, b, number)
                    number += 1
                    quantise_waiting(number)
                    if (b + 1) % chunk == 0:
                        waiting.append((number + Q_DELAY, n, b + 1 - chunk, chunk))
                    if b == banks_of(n) - 1 and n + RAW_BUFS < len(PIECES):
                        load(n + RAW_BUFS)
                    if number % RUN_BANKS == 0:
                        due = passes_due(number)
                        if PIECES[PASSES[done][2]][0] == 0:
                            due = len(PASSES)
                        while done < due and is_ready(done):
                            multiply_pass(done)
                            done += 1
            quantise_waiting(ALL_BANKS + Q_DELAY)
            tiles_of = [[i for i in range(X_TILES) if i // 2 == j] for j in range(PAIRS)]
            for j in range(PAIRS + 2):
                if j < PAIRS:
                    for q in range(done, LAST_PASS[j] + 1):
                        multiply_pass(q)
                    done = max(done, LAST_PASS[j] + 1)
                    for i in tiles_of[j]:
                        sum_squares(i)
                if 1 <= j <= PAIRS:
                    for i in tiles_of[j - 1]:
                        invert(i)
                if j >= 2:
                    for i in tiles_of[j - 2]:
                        scale_and_store(i)
